import numpy as np
import ml_dtypes


def mxq(x, axis, fmt="e4m3"):
    dtype, down = {"e4m3": (ml_dtypes.float8_e4m3fn, 7), "e5m2": (ml_dtypes.float8_e5m2, 14)}[fmt]
    v = np.moveaxis(np.asarray(x, np.float32).astype(ml_dtypes.bfloat16).astype(np.float64), axis, -1)
    blocks = v.reshape(v.shape[:-1] + (-1, 32))
    amax = np.abs(blocks).max(-1, keepdims=True)
    byte = np.maximum(np.where(amax > 0, np.frexp(amax)[1] - 1 + 127, 0) - down, 1)
    scale = np.exp2(byte - 127.0)
    codes = (blocks / scale).astype(np.float32).astype(dtype).astype(np.float64)
    return np.moveaxis((codes * scale).reshape(v.shape), -1, axis)


WIDE = False


def mx_kscale(k):
    if not WIDE:
        return np.ones(k)
    levels = np.array([10, -10, 5, -5, 0])
    a = np.random.permutation(np.resize(levels, k // 512 * 4)).reshape(k // 512, 4)
    idx = np.arange(k)
    return np.exp2(a[idx // 512, idx % 128 // 32])


BF16 = ml_dtypes.bfloat16


def bf(x):
    return np.asarray(x, np.float32).astype(BF16)


def f64(x):
    return np.asarray(x).astype(np.float64)


E2M1 = np.array([0.0, 0.5, 1.0, 1.5, 2.0, 3.0, 4.0, 6.0, -0.0, -0.5, -1.0, -1.5, -2.0, -3.0, -4.0, -6.0])


def pack_weight(w, fmt):
    k, n = w.shape
    w = f64(bf(w)).reshape(k // 32, 32, n)
    amax = np.abs(w).max(1)
    if fmt == "e4m3":
        byte = np.frexp(amax)[1] - 1 + 127 - 7
    else:
        mant, ex = np.frexp(amax / 6.0)
        byte = np.where(mant > 0.5, ex, ex - 1) + 127
    byte = np.clip(np.where(amax > 0, byte, 1), 1, 254)
    scaled = (w * np.exp2(127.0 - byte)[:, None, :]).reshape(k, n).astype(np.float32)
    by_word = np.ascontiguousarray(scaled.reshape(k // 512, 128, 4, n).transpose(0, 1, 3, 2))
    if fmt == "e4m3":
        words = by_word.astype(ml_dtypes.float8_e4m3fn).view(np.uint8)
    else:
        c = by_word.astype(ml_dtypes.float4_e2m1fn).view(np.uint8) & 0xF
        words = c[..., 0::2] | (c[..., 1::2] << 4)
    return np.ascontiguousarray(words), np.ascontiguousarray(byte.astype(np.uint8).reshape(k // 512, 16, n))


def unpack_weight(words, scales, fmt):
    g, p, n, _ = words.shape
    if fmt == "e4m3":
        vals = np.ascontiguousarray(words).view(ml_dtypes.float8_e4m3fn).astype(np.float64)
    else:
        nib = np.empty((g, p, n, 4), np.uint8)
        nib[..., 0::2] = words & 0xF
        nib[..., 1::2] = words >> 4
        vals = E2M1[nib]
    vals = vals * np.repeat(np.exp2(scales.astype(np.float64) - 127.0), 8, axis=1)[..., None]
    return vals.transpose(0, 1, 3, 2).reshape(g * 512, n)

def pack4(w):
    words, scales = pack_weight(w, "e2m1")
    return words.reshape(words.shape[0], 128, -1), scales


def unpack4(words, scales):
    return unpack_weight(words.reshape(words.shape[0], 128, -1, 2), scales, "e2m1")


B, T, D, H, HD = 2, 512, 1024, 8, 128
E = H * HD


def rope(u):
    inv_freq = 1.0 / (10000.0 ** (f64(np.arange(0, HD, 2)) / HD))
    pe = f64(np.arange(T))[:, None] * inv_freq[None, :]
    pe = np.repeat(pe, 2, axis=-1)
    u1 = u[..., 0::2]
    u2 = u[..., 1::2]
    rot = np.stack((-u2, u1), axis=-1).reshape(u.shape)
    return u * np.cos(pe) + rot * np.sin(pe)


def split_heads(u):
    return u.reshape(B, T, H, HD).transpose(0, 2, 1, 3)


def setup_inputs():
    s = mx_kscale(D)
    x = bf(np.random.standard_normal((B, T, D)) * s)
    words, scales = pack4(np.random.standard_normal((D, 3 * E)) / np.sqrt(D) / s[:, None])
    return {"x": x, "w_qkv_words": words, "w_qkv_scales": scales}


def reference(x, w_qkv_words, w_qkv_scales):
    qkv = mxq(f64(x), 2, "e4m3") @ unpack4(w_qkv_words, w_qkv_scales)
    q, k, v = np.split(qkv, 3, axis=2)
    q, k, v = split_heads(q), split_heads(k), split_heads(v)
    return rope(q), rope(k), v

@@ -1,0 +1,231 @@
+import math
+from contextlib import ExitStack
+
+import concourse.mybir as mybir
+from concourse.masks import make_identity
+
+F32 = mybir.dt.float32
+BF16 = mybir.dt.bfloat16
+I32 = mybir.dt.int32
+U32 = mybir.dt.uint32
+U8 = mybir.dt.uint8
+FP8X4 = mybir.dt.float8_e4m3fn_x4
+FP4X4 = mybir.dt.float4_e2m1fn_x4
+MULT = mybir.AluOpType.mult
+ADD = mybir.AluOpType.add
+SUBTRACT = mybir.AluOpType.subtract
+MAX = mybir.AluOpType.max
+SIN = mybir.ActivationFunctionType.Sin
+
+B, T, D, H, HD = 2, 512, 1024, 8, 128
+E = H * HD
+P = 128
+PACK = 4
+K_PASS = P * PACK
+PASSES = D // K_PASS
+TOK = T // P
+N_TILE = 512
+GROUP_HEADS = N_TILE // HD
+HEAD_GROUPS = H // GROUP_HEADS
+PAIRS = HD // 2
+DOUBLINGS = 6
+assert 2**DOUBLINGS == PAIRS
+ROUND_MAGIC = 1.5 * 2.0**23
+
+FLOPS = 2 * B * T * D * 3 * E
+
+
+def build_rotation_tables(nc, keep):
+    position_int = keep.tile([P, TOK], I32)
+    nc.gpsimd.iota(position_int[:], pattern=[[1, TOK]], base=0, channel_multiplier=TOK)
+    position = keep.tile([P, TOK], F32)
+    nc.vector.tensor_copy(out=position[:], in_=position_int[:])
+
+    freq = keep.tile([P, PAIRS], F32)
+    nc.vector.memset(freq[:, 0:1], 1.0)
+    for doubling in range(DOUBLINGS):
+        have = 2**doubling
+        nc.vector.tensor_scalar_mul(
+            out=freq[:, have : 2 * have], in0=freq[:, 0:have], scalar1=10000.0 ** (-2.0 * have / HD)
+        )
+
+    shape = [P, TOK, PAIRS]
+    turns = keep.tile(shape, F32)
+    nc.vector.scalar_tensor_tensor(
+        out=turns[:],
+        in0=freq[:].unsqueeze(1).to_broadcast(shape),
+        scalar=1.0 / (2.0 * math.pi),
+        in1=position[:].unsqueeze(2).to_broadcast(shape),
+        op0=MULT,
+        op1=MULT,
+    )
+    whole = keep.tile(shape, F32)
+    nc.vector.tensor_scalar(
+        out=whole[:], in0=turns[:], scalar1=ROUND_MAGIC, scalar2=ROUND_MAGIC, op0=ADD, op1=SUBTRACT
+    )
+    part = keep.tile(shape, F32)
+    nc.vector.tensor_tensor(out=part[:], in0=turns[:], in1=whole[:], op=SUBTRACT)
+    size = keep.tile(shape, F32)
+    nc.vector.scalar_tensor_tensor(
+        out=size[:], in0=part[:], scalar=-1.0, in1=part[:], op0=MULT, op1=MAX
+    )
+    quarter_less = keep.tile(shape, F32)
+    nc.vector.tensor_scalar(
+        out=quarter_less[:], in0=size[:], scalar1=-1.0, scalar2=0.25, op0=MULT, op1=ADD
+    )
+
+    sin = keep.tile(shape, F32)
+    nc.scalar.activation(out=sin[:], in_=part[:], func=SIN, scale=2.0 * math.pi)
+    neg_sin = keep.tile(shape, F32)
+    nc.scalar.activation(out=neg_sin[:], in_=part[:], func=SIN, scale=-2.0 * math.pi)
+    cos = keep.tile([P, TOK, PAIRS, 2], F32)
+    nc.scalar.activation(
+        out=cos[:],
+        in_=quarter_less[:].unsqueeze(3).to_broadcast([P, TOK, PAIRS, 2]),
+        func=SIN,
+        scale=2.0 * math.pi,
+    )
+    return cos, sin, neg_sin
+
+
+def tile_selfattention_pa_kernel(tc, x, w_qkv_words, w_qkv_scales, out_0, out_1, out_2):
+    nc = tc.nc
+    with ExitStack() as pools:
+        keep = pools.enter_context(tc.tile_pool(name="keep", bufs=1))
+        stage = pools.enter_context(tc.tile_pool(name="stage", bufs=2))
+        products = pools.enter_context(tc.tile_pool(name="products", bufs=3))
+        results = pools.enter_context(tc.tile_pool(name="results", bufs=4))
+        flipped = pools.enter_context(tc.psum_pool(name="flipped", bufs=2))
+        sums = pools.enter_context(tc.psum_pool(name="sums", bufs=6))
+
+        outputs = ((out_0, 0, True), (out_2, 2, False), (out_1, 1, True))
+
+        x_rows = keep.tile([P, B, TOK, D], BF16)
+        x_by_partition = x.rearrange("b (p j) k -> b p j k", j=TOK)
+
+        def load_x(b, j):
+            nc.sync.dma_start(out=x_rows[:, b, j, :], in_=x_by_partition[b, :, j, :])
+
+        w_words = keep.tile([P, PASSES, 2 * 3 * E], U8, align_bytes=64)
+        words_by_partition = w_qkv_words.rearrange("g p n -> p g n")
+
+        def load_w(chunk):
+            cols = slice(2 * N_TILE * chunk, 2 * N_TILE * (chunk + 1))
+            nc.sync.dma_start(
+                out=w_words[:, :, cols].bitcast(I32), in_=words_by_partition[:, :, cols].bitcast(I32)
+            )
+
+        w_scales = keep.tile([P, PASSES, 3 * E], U8, align_bytes=64)
+        nc.vector.memset(w_scales[:].bitcast(I32), 0)
+        scales_by_row = w_qkv_scales.rearrange("g q n -> q g n")
+
+        chunk_order = [
+            third * HEAD_GROUPS + group for group in range(HEAD_GROUPS) for (dst, third, rotated) in outputs
+        ]
+        load_x(0, 0)
+        load_w(chunk_order[0])
+        for r in range(4):
+            nc.sync.dma_start(out=w_scales[r:P:32].bitcast(I32), in_=scales_by_row[r:16:4].bitcast(I32))
+        for j in range(1, TOK):
+            load_x(0, j)
+        for chunk in chunk_order[1:]:
+            load_w(chunk)
+        for b in range(1, B):
+            for j in range(TOK):
+                load_x(b, j)
+
+        identity = keep.tile([P, P], F32)
+        make_identity(nc, identity[:])
+        cos, sin, neg_sin = build_rotation_tables(nc, keep)
+
+        x_codes = keep.tile([P, B, TOK, PASSES, P], U32, align_bytes=64)
+        x_scales = keep.tile([P, B, TOK, PASSES, P], U8, align_bytes=64)
+
+        def quantise_positions(b, j):
+            words = x_rows[:, b, j, :].bitcast(F32)
+            turned = flipped.tile([P, PASSES, 2, P], F32)
+            for g in range(PASSES):
+                for u in range(2):
+                    nc.tensor.transpose(
+                        turned[:, g, u, :], words[:, 2 * P * g + u : 2 * P * (g + 1) : 2], identity[:]
+                    )
+            grouped = stage.tile([P, PASSES, P, PACK], BF16, align_bytes=64)
+            nc.scalar.copy(
+                out=grouped[:]
+                .rearrange("p g r t -> p (g r t)")
+                .bitcast(F32)
+                .rearrange("p (g r u) -> p g r u", g=PASSES, u=2),
+                in_=turned[:].rearrange("p g u r -> p g r u"),
+            )
+            nc.vector.quantize_mx(
+                out=x_codes[:, b, j].rearrange("p g r -> p (g r)").bitcast(FP8X4),
+                scales=x_scales[:, b, j].rearrange("p g r -> p (g r)"),
+                in_=grouped[:].rearrange("p g r t -> p (g r t)"),
+            )
+
+        def rotate(acc, j, rotated_out):
+            by_head = [P, GROUP_HEADS, HD]
+            by_pair = [P, GROUP_HEADS, PAIRS]
+            pairs = acc[:].rearrange("p (h i e) -> p h i e", h=GROUP_HEADS, e=2)
+            straight = products.tile([P, GROUP_HEADS, PAIRS, 2], F32)
+            nc.vector.tensor_tensor(
+                out=straight[:].rearrange("p h i e -> p h (i e)"),
+                in0=acc[:].rearrange("p (h d) -> p h d", d=HD),
+                in1=cos[:, j].rearrange("p i e -> p (i e)").unsqueeze(1).to_broadcast(by_head),
+                op=MULT,
+            )
+            crossed = products.tile([P, 2, GROUP_HEADS, PAIRS], F32)
+            nc.vector.tensor_tensor(
+                out=crossed[:, 0],
+                in0=pairs[:, :, :, 1],
+                in1=neg_sin[:, j].unsqueeze(1).to_broadcast(by_pair),
+                op=MULT,
+            )
+            nc.vector.tensor_tensor(
+                out=crossed[:, 1],
+                in0=pairs[:, :, :, 0],
+                in1=sin[:, j].unsqueeze(1).to_broadcast(by_pair),
+                op=MULT,
+            )
+            nc.gpsimd.tensor_tensor(
+                out=rotated_out.rearrange("p h (i e) -> p h i e", e=2),
+                in0=straight[:],
+                in1=crossed[:].rearrange("p e h i -> p h i e"),
+                op=ADD,
+            )
+
+        for j in range(TOK):
+            quantise_positions(0, j)
+
+        for b in range(B):
+            done = 0
+            for group in range(HEAD_GROUPS):
+                heads = slice(GROUP_HEADS * group, GROUP_HEADS * (group + 1))
+                for dst, third, rotated in outputs:
+                    chunk = third * HEAD_GROUPS + group
+                    result = results.tile([P, GROUP_HEADS, TOK, HD], F32)
+                    for j in range(TOK):
+                        acc = sums.tile([P, N_TILE], F32)
+                        for g in range(PASSES):
+                            nc.tensor.matmul_mx(
+                                out=acc[:],
+                                lhsT=x_codes[:, b, j, g, :].bitcast(FP8X4),
+                                lhsT_scale=x_scales[:, b, j, g, :],
+                                rhs=w_words[:, g, 2 * N_TILE * chunk : 2 * N_TILE * (chunk + 1)].bitcast(FP4X4),
+                                rhs_scale=w_scales[:, g, N_TILE * chunk : N_TILE * (chunk + 1)],
+                                start=(g == 0),
+                                stop=(g == PASSES - 1),
+                            )
+                        if rotated:
+                            rotate(acc, j, result[:, :, j, :])
+                        else:
+                            nc.scalar.copy(
+                                out=result[:, :, j, :], in_=acc[:].rearrange("p (h d) -> p h d", d=HD)
+                            )
+                    nc.sync.dma_start(
+                        out=dst[b, heads].rearrange("h (p j) d -> p h (j d)", j=TOK),
+                        in_=result[:].rearrange("p h j d -> p h (j d)"),
+                    )
+                    if b + 1 < B and done < TOK:
+                        quantise_positions(b + 1, done)
+                    done += 1

@@ -74,18 +74,12 @@ def build_rotation_tables(nc, keep):
         out=quarter_less[:], in0=size[:], scalar1=-1.0, scalar2=0.25, op0=MULT, op1=ADD
     )
 
-    sin = keep.tile(shape, F32)
-    nc.scalar.activation(out=sin[:], in_=part[:], func=SIN, scale=2.0 * math.pi)
-    neg_sin = keep.tile(shape, F32)
-    nc.scalar.activation(out=neg_sin[:], in_=part[:], func=SIN, scale=-2.0 * math.pi)
-    cos = keep.tile([P, TOK, PAIRS, 2], F32)
-    nc.scalar.activation(
-        out=cos[:],
-        in_=quarter_less[:].unsqueeze(3).to_broadcast([P, TOK, PAIRS, 2]),
-        func=SIN,
-        scale=2.0 * math.pi,
-    )
-    return cos, sin, neg_sin
+    table = keep.tile([P, TOK, 2, PAIRS, 2], F32)
+    nc.scalar.activation(out=table[:, :, 0, :, 1], in_=part[:], func=SIN, scale=2.0 * math.pi)
+    nc.scalar.activation(out=table[:, :, 1, :, 0], in_=part[:], func=SIN, scale=-2.0 * math.pi)
+    for w in range(2):
+        nc.scalar.activation(out=table[:, :, w, :, w], in_=quarter_less[:], func=SIN, scale=2.0 * math.pi)
+    return table
 
 
 def tile_selfattention_pa_kernel(tc, x, w_qkv_words, w_qkv_scales, out_0, out_1, out_2):
@@ -136,7 +130,7 @@ def tile_selfattention_pa_kernel(tc, x, w_qkv_words, w_qkv_scales, out_0, out_1,
 
         identity = keep.tile([P, P], F32)
         make_identity(nc, identity[:])
-        cos, sin, neg_sin = build_rotation_tables(nc, keep)
+        table = build_rotation_tables(nc, keep)
 
         x_codes = keep.tile([P, B, TOK, PASSES, P], U32, align_bytes=64)
         x_scales = keep.tile([P, B, TOK, PASSES, P], U8, align_bytes=64)
@@ -163,35 +157,13 @@ def tile_selfattention_pa_kernel(tc, x, w_qkv_words, w_qkv_scales, out_0, out_1,
                 in_=grouped[:].rearrange("p g r t -> p (g r t)"),
             )
 
-        def rotate(acc, j, rotated_out):
-            by_head = [P, GROUP_HEADS, HD]
-            by_pair = [P, GROUP_HEADS, PAIRS]
-            pairs = acc[:].rearrange("p (h i e) -> p h i e", h=GROUP_HEADS, e=2)
-            straight = products.tile([P, GROUP_HEADS, PAIRS, 2], F32)
+        def multiply(acc, j, both):
+            shape = [P, 2, GROUP_HEADS, PAIRS, 2]
             nc.vector.tensor_tensor(
-                out=straight[:].rearrange("p h i e -> p h (i e)"),
-                in0=acc[:].rearrange("p (h d) -> p h d", d=HD),
-                in1=cos[:, j].rearrange("p i e -> p (i e)").unsqueeze(1).to_broadcast(by_head),
+                out=both[:, :, :, j, :].rearrange("p w h (i e) -> p w h i e", e=2),
+                in0=acc[:].rearrange("p (h i w) -> p w h i", h=GROUP_HEADS, w=2).unsqueeze(4).to_broadcast(shape),
+                in1=table[:, j].unsqueeze(2).to_broadcast(shape),
                 op=MULT,
-            )
-            crossed = products.tile([P, 2, GROUP_HEADS, PAIRS], F32)
-            nc.vector.tensor_tensor(
-                out=crossed[:, 0],
-                in0=pairs[:, :, :, 1],
-                in1=neg_sin[:, j].unsqueeze(1).to_broadcast(by_pair),
-                op=MULT,
-            )
-            nc.vector.tensor_tensor(
-                out=crossed[:, 1],
-                in0=pairs[:, :, :, 0],
-                in1=sin[:, j].unsqueeze(1).to_broadcast(by_pair),
-                op=MULT,
-            )
-            nc.gpsimd.tensor_tensor(
-                out=rotated_out.rearrange("p h (i e) -> p h i e", e=2),
-                in0=straight[:],
-                in1=crossed[:].rearrange("p e h i -> p h i e"),
-                op=ADD,
             )
 
         for j in range(TOK):
@@ -204,6 +176,8 @@ def tile_selfattention_pa_kernel(tc, x, w_qkv_words, w_qkv_scales, out_0, out_1,
                 for dst, third, rotated in outputs:
                     chunk = third * HEAD_GROUPS + group
                     result = results.tile([P, GROUP_HEADS, TOK, HD], F32)
+                    if rotated:
+                        both = products.tile([P, 2, GROUP_HEADS, TOK, HD], F32)
                     for j in range(TOK):
                         acc = sums.tile([P, N_TILE], F32)
                         for g in range(PASSES):
@@ -217,11 +191,18 @@ def tile_selfattention_pa_kernel(tc, x, w_qkv_words, w_qkv_scales, out_0, out_1,
                                 stop=(g == PASSES - 1),
                             )
                         if rotated:
-                            rotate(acc, j, result[:, :, j, :])
+                            multiply(acc, j, both)
                         else:
                             nc.scalar.copy(
                                 out=result[:, :, j, :], in_=acc[:].rearrange("p (h d) -> p h d", d=HD)
                             )
+                    if rotated:
+                        nc.gpsimd.tensor_tensor(
+                            out=result[:].rearrange("p h j d -> p (h j d)"),
+                            in0=both[:, 0].rearrange("p h j d -> p (h j d)"),
+                            in1=both[:, 1].rearrange("p h j d -> p (h j d)"),
+                            op=ADD,
+                        )
                     nc.sync.dma_start(
                         out=dst[b, heads].rearrange("h (p j) d -> p h (j d)", j=TOK),
                         in_=result[:].rearrange("p h j d -> p h (j d)"),

@@ -35,7 +35,7 @@ ROUND_MAGIC = 1.5 * 2.0**23
 FLOPS = 2 * B * T * D * 3 * E
 
 
-def build_rotation_tables(nc, keep):
+def build_angles(nc, keep):
     position_int = keep.tile([P, TOK], I32)
     nc.gpsimd.iota(position_int[:], pattern=[[1, TOK]], base=0, channel_multiplier=TOK)
     position = keep.tile([P, TOK], F32)
@@ -74,6 +74,10 @@ def build_rotation_tables(nc, keep):
         out=quarter_less[:], in0=size[:], scalar1=-1.0, scalar2=0.25, op0=MULT, op1=ADD
     )
 
+    return part, quarter_less
+
+
+def build_rotation_table(nc, keep, part, quarter_less):
     table = keep.tile([P, TOK, 2, PAIRS, 2], F32)
     nc.scalar.activation(out=table[:, :, 0, :, 1], in_=part[:], func=SIN, scale=2.0 * math.pi)
     nc.scalar.activation(out=table[:, :, 1, :, 0], in_=part[:], func=SIN, scale=-2.0 * math.pi)
@@ -86,13 +90,23 @@ def tile_selfattention_pa_kernel(tc, x, w_qkv_words, w_qkv_scales, out_0, out_1,
     nc = tc.nc
     with ExitStack() as pools:
         keep = pools.enter_context(tc.tile_pool(name="keep", bufs=1))
-        stage = pools.enter_context(tc.tile_pool(name="stage", bufs=2))
+        stage = pools.enter_context(tc.tile_pool(name="stage", bufs=3))
         products = pools.enter_context(tc.tile_pool(name="products", bufs=3))
         results = pools.enter_context(tc.tile_pool(name="results", bufs=4))
         flipped = pools.enter_context(tc.psum_pool(name="flipped", bufs=2))
         sums = pools.enter_context(tc.psum_pool(name="sums", bufs=6))
+        pools.enter_context(tc.manual_schedule())
 
-        outputs = ((out_0, 0, True), (out_2, 2, False), (out_1, 1, True))
+        pieces = [
+            (b, group, dst, third, rotated)
+            for b in range(B)
+            for group in range(HEAD_GROUPS)
+            for (dst, third, rotated) in ((out_0, 0, True), (out_2, 2, False), (out_1, 1, True))
+        ]
+
+        warm = keep.tile([P, 2], F32)
+        nc.vector.memset(warm[:, 0:1], 0.0)
+        nc.scalar.activation(out=warm[:, 1:2], in_=warm[:, 0:1], func=SIN)
 
         x_rows = keep.tile([P, B, TOK, D], BF16)
         x_by_partition = x.rearrange("b (p j) k -> b p j k", j=TOK)
@@ -113,24 +127,21 @@ def tile_selfattention_pa_kernel(tc, x, w_qkv_words, w_qkv_scales, out_0, out_1,
         nc.vector.memset(w_scales[:].bitcast(I32), 0)
         scales_by_row = w_qkv_scales.rearrange("g q n -> q g n")
 
-        chunk_order = [
-            third * HEAD_GROUPS + group for group in range(HEAD_GROUPS) for (dst, third, rotated) in outputs
-        ]
+        chunk_order = [third * HEAD_GROUPS + group for (b, group, dst, third, rotated) in pieces if b == 0]
         load_x(0, 0)
         load_w(chunk_order[0])
         for r in range(4):
             nc.sync.dma_start(out=w_scales[r:P:32].bitcast(I32), in_=scales_by_row[r:16:4].bitcast(I32))
-        for j in range(1, TOK):
-            load_x(0, j)
+        for b in range(B):
+            for j in range(TOK):
+                if (b, j) != (0, 0):
+                    load_x(b, j)
         for chunk in chunk_order[1:]:
             load_w(chunk)
-        for b in range(1, B):
-            for j in range(TOK):
-                load_x(b, j)
 
+        part, quarter_less = build_angles(nc, keep)
         identity = keep.tile([P, P], F32)
         make_identity(nc, identity[:])
-        table = build_rotation_tables(nc, keep)
 
         x_codes = keep.tile([P, B, TOK, PASSES, P], U32, align_bytes=64)
         x_scales = keep.tile([P, B, TOK, PASSES, P], U8, align_bytes=64)
@@ -157,6 +168,22 @@ def tile_selfattention_pa_kernel(tc, x, w_qkv_words, w_qkv_scales, out_0, out_1,
                 in_=grouped[:].rearrange("p g r t -> p (g r t)"),
             )
 
+        def project(piece, j):
+            b, group, dst, third, rotated = piece
+            chunk = third * HEAD_GROUPS + group
+            acc = sums.tile([P, N_TILE], F32)
+            for g in range(PASSES):
+                nc.tensor.matmul_mx(
+                    out=acc[:],
+                    lhsT=x_codes[:, b, j, g, :].bitcast(FP8X4),
+                    lhsT_scale=x_scales[:, b, j, g, :],
+                    rhs=w_words[:, g, 2 * N_TILE * chunk : 2 * N_TILE * (chunk + 1)].bitcast(FP4X4),
+                    rhs_scale=w_scales[:, g, N_TILE * chunk : N_TILE * (chunk + 1)],
+                    start=(g == 0),
+                    stop=(g == PASSES - 1),
+                )
+            return acc
+
         def multiply(acc, j, both):
             shape = [P, 2, GROUP_HEADS, PAIRS, 2]
             nc.vector.tensor_tensor(
@@ -166,47 +193,62 @@ def tile_selfattention_pa_kernel(tc, x, w_qkv_words, w_qkv_scales, out_0, out_1,
                 op=MULT,
             )
 
-        for j in range(TOK):
-            quantise_positions(0, j)
+        def store(queue, piece, result):
+            b, group, dst, third, rotated = piece
+            heads = slice(GROUP_HEADS * group, GROUP_HEADS * (group + 1))
+            queue.dma_start(
+                out=dst[b, heads].rearrange("h (p j) d -> p h (j d)", j=TOK),
+                in_=result[:].rearrange("p h j d -> p h (j d)"),
+            )
 
-        for b in range(B):
-            done = 0
-            for group in range(HEAD_GROUPS):
-                heads = slice(GROUP_HEADS * group, GROUP_HEADS * (group + 1))
-                for dst, third, rotated in outputs:
-                    chunk = third * HEAD_GROUPS + group
+        def store_positions(piece, result, j):
+            b, group, dst, third, rotated = piece
+            heads = slice(GROUP_HEADS * group, GROUP_HEADS * (group + 1))
+            nc.sync.dma_start(
+                out=dst[b, heads].rearrange("h (p j) d -> p h j d", j=TOK)[:, :, j, :], in_=result[:, :, j, :]
+            )
+
+        def add_all(piece, both):
+            result = results.tile([P, GROUP_HEADS, TOK, HD], F32)
+            nc.gpsimd.tensor_tensor(
+                out=result[:].rearrange("p h j d -> p (h j d)"),
+                in0=both[:, 0].rearrange("p h j d -> p (h j d)"),
+                in1=both[:, 1].rearrange("p h j d -> p (h j d)"),
+                op=ADD,
+            )
+            store(nc.sync, piece, result)
+
+        both = products.tile([P, 2, GROUP_HEADS, TOK, HD], F32)
+        waiting = []
+        quantise_positions(0, 0)
+        table = build_rotation_table(nc, keep, part, quarter_less)
+        for step in range(1, B * TOK):
+            quantise_positions(step // TOK, step % TOK)
+            if 3 <= step < 3 + TOK:
+                waiting.append(project(pieces[0], step - 3))
+            if 4 <= step < 3 + TOK:
+                multiply(waiting[step - 4], step - 4, both)
+        multiply(waiting[TOK - 1], TOK - 1, both)
+        add_all(pieces[0], both)
+
+        for piece in pieces[1:]:
+            rotated = piece[4]
+            if rotated:
+                both = products.tile([P, 2, GROUP_HEADS, TOK, HD], F32)
+                for j in range(TOK):
+                    multiply(project(piece, j), j, both)
+                if piece is not pieces[-1]:
+                    add_all(piece, both)
+                else:
                     result = results.tile([P, GROUP_HEADS, TOK, HD], F32)
-                    if rotated:
-                        both = products.tile([P, 2, GROUP_HEADS, TOK, HD], F32)
                     for j in range(TOK):
-                        acc = sums.tile([P, N_TILE], F32)
-                        for g in range(PASSES):
-                            nc.tensor.matmul_mx(
-                                out=acc[:],
-                                lhsT=x_codes[:, b, j, g, :].bitcast(FP8X4),
-                                lhsT_scale=x_scales[:, b, j, g, :],
-                                rhs=w_words[:, g, 2 * N_TILE * chunk : 2 * N_TILE * (chunk + 1)].bitcast(FP4X4),
-                                rhs_scale=w_scales[:, g, N_TILE * chunk : N_TILE * (chunk + 1)],
-                                start=(g == 0),
-                                stop=(g == PASSES - 1),
-                            )
-                        if rotated:
-                            multiply(acc, j, both)
-                        else:
-                            nc.scalar.copy(
-                                out=result[:, :, j, :], in_=acc[:].rearrange("p (h d) -> p h d", d=HD)
-                            )
-                    if rotated:
-                        nc.gpsimd.tensor_tensor(
-                            out=result[:].rearrange("p h j d -> p (h j d)"),
-                            in0=both[:, 0].rearrange("p h j d -> p (h j d)"),
-                            in1=both[:, 1].rearrange("p h j d -> p (h j d)"),
-                            op=ADD,
+                        nc.vector.tensor_tensor(
+                            out=result[:, :, j, :], in0=both[:, 0, :, j, :], in1=both[:, 1, :, j, :], op=ADD
                         )
-                    nc.sync.dma_start(
-                        out=dst[b, heads].rearrange("h (p j) d -> p h (j d)", j=TOK),
-                        in_=result[:].rearrange("p h j d -> p h (j d)"),
-                    )
-                    if b + 1 < B and done < TOK:
-                        quantise_positions(b + 1, done)
-                    done += 1
+                        store_positions(piece, result, j)
+            else:
+                result = results.tile([P, GROUP_HEADS, TOK, HD], F32)
+                for j in range(TOK):
+                    acc = project(piece, j)
+                    nc.scalar.copy(out=result[:, :, j, :], in_=acc[:].rearrange("p (h d) -> p h d", d=HD))
+                store(nc.scalar, piece, result)

@@ -32,6 +32,8 @@ DOUBLINGS = 6
 assert 2**DOUBLINGS == PAIRS
 ROUND_MAGIC = 1.5 * 2.0**23
 
+ROTATED_PIECES = 2 * B * HEAD_GROUPS
+
 FLOPS = 2 * B * T * D * 3 * E
 
 
@@ -90,11 +92,10 @@ def tile_selfattention_pa_kernel(tc, x, w_qkv_words, w_qkv_scales, out_0, out_1,
     nc = tc.nc
     with ExitStack() as pools:
         keep = pools.enter_context(tc.tile_pool(name="keep", bufs=1))
-        stage = pools.enter_context(tc.tile_pool(name="stage", bufs=3))
-        products = pools.enter_context(tc.tile_pool(name="products", bufs=3))
-        results = pools.enter_context(tc.tile_pool(name="results", bufs=4))
-        flipped = pools.enter_context(tc.psum_pool(name="flipped", bufs=2))
-        sums = pools.enter_context(tc.psum_pool(name="sums", bufs=6))
+        stage = pools.enter_context(tc.tile_pool(name="stage", bufs=4))
+        products = pools.enter_context(tc.tile_pool(name="products", bufs=4))
+        results = pools.enter_context(tc.tile_pool(name="results", bufs=5))
+        banks = pools.enter_context(tc.psum_pool(name="banks", bufs=8))
         pools.enter_context(tc.manual_schedule())
 
         pieces = [
@@ -132,12 +133,12 @@ def tile_selfattention_pa_kernel(tc, x, w_qkv_words, w_qkv_scales, out_0, out_1,
         load_w(chunk_order[0])
         for r in range(4):
             nc.sync.dma_start(out=w_scales[r:P:32].bitcast(I32), in_=scales_by_row[r:16:4].bitcast(I32))
-        for b in range(B):
-            for j in range(TOK):
-                if (b, j) != (0, 0):
-                    load_x(b, j)
+        for j in range(1, TOK):
+            load_x(0, j)
         for chunk in chunk_order[1:]:
             load_w(chunk)
+        for j in range(TOK):
+            load_x(1, j)
 
         part, quarter_less = build_angles(nc, keep)
         identity = keep.tile([P, P], F32)
@@ -146,9 +147,9 @@ def tile_selfattention_pa_kernel(tc, x, w_qkv_words, w_qkv_scales, out_0, out_1,
         x_codes = keep.tile([P, B, TOK, PASSES, P], U32, align_bytes=64)
         x_scales = keep.tile([P, B, TOK, PASSES, P], U8, align_bytes=64)
 
-        def quantise_positions(b, j):
+        def prepare(b, j):
             words = x_rows[:, b, j, :].bitcast(F32)
-            turned = flipped.tile([P, PASSES, 2, P], F32)
+            turned = banks.tile([P, PASSES, 2, P], F32, tag="bank")
             for g in range(PASSES):
                 for u in range(2):
                     nc.tensor.transpose(
@@ -162,6 +163,9 @@ def tile_selfattention_pa_kernel(tc, x, w_qkv_words, w_qkv_scales, out_0, out_1,
                 .rearrange("p (g r u) -> p g r u", g=PASSES, u=2),
                 in_=turned[:].rearrange("p g u r -> p g r u"),
             )
+            return grouped
+
+        def quantise(b, j, grouped):
             nc.vector.quantize_mx(
                 out=x_codes[:, b, j].rearrange("p g r -> p (g r)").bitcast(FP8X4),
                 scales=x_scales[:, b, j].rearrange("p g r -> p (g r)"),
@@ -171,7 +175,7 @@ def tile_selfattention_pa_kernel(tc, x, w_qkv_words, w_qkv_scales, out_0, out_1,
         def project(piece, j):
             b, group, dst, third, rotated = piece
             chunk = third * HEAD_GROUPS + group
-            acc = sums.tile([P, N_TILE], F32)
+            acc = banks.tile([P, N_TILE], F32, tag="bank")
             for g in range(PASSES):
                 nc.tensor.matmul_mx(
                     out=acc[:],
@@ -193,62 +197,65 @@ def tile_selfattention_pa_kernel(tc, x, w_qkv_words, w_qkv_scales, out_0, out_1,
                 op=MULT,
             )
 
-        def store(queue, piece, result):
+        def store(queue, piece, result, first, count):
             b, group, dst, third, rotated = piece
             heads = slice(GROUP_HEADS * group, GROUP_HEADS * (group + 1))
             queue.dma_start(
-                out=dst[b, heads].rearrange("h (p j) d -> p h (j d)", j=TOK),
-                in_=result[:].rearrange("p h j d -> p h (j d)"),
+                out=dst[b, heads].rearrange("h (p j) d -> p h j d", j=TOK)[:, :, first : first + count, :],
+                in_=result[:, :, first : first + count, :],
             )
 
-        def store_positions(piece, result, j):
-            b, group, dst, third, rotated = piece
-            heads = slice(GROUP_HEADS * group, GROUP_HEADS * (group + 1))
-            nc.sync.dma_start(
-                out=dst[b, heads].rearrange("h (p j) d -> p h j d", j=TOK)[:, :, j, :], in_=result[:, :, j, :]
-            )
-
-        def add_all(piece, both):
-            result = results.tile([P, GROUP_HEADS, TOK, HD], F32)
-            nc.gpsimd.tensor_tensor(
-                out=result[:].rearrange("p h j d -> p (h j d)"),
-                in0=both[:, 0].rearrange("p h j d -> p (h j d)"),
-                in1=both[:, 1].rearrange("p h j d -> p (h j d)"),
+        def add(engine, both, result, first, count):
+            engine.tensor_tensor(
+                out=result[:, :, first : first + count, :],
+                in0=both[:, 0, :, first : first + count, :],
+                in1=both[:, 1, :, first : first + count, :],
                 op=ADD,
             )
-            store(nc.sync, piece, result)
 
         both = products.tile([P, 2, GROUP_HEADS, TOK, HD], F32)
-        waiting = []
-        quantise_positions(0, 0)
+        quantise(0, 0, prepare(0, 0))
         table = build_rotation_table(nc, keep, part, quarter_less)
-        for step in range(1, B * TOK):
-            quantise_positions(step // TOK, step % TOK)
-            if 3 <= step < 3 + TOK:
-                waiting.append(project(pieces[0], step - 3))
-            if 4 <= step < 3 + TOK:
-                multiply(waiting[step - 4], step - 4, both)
-        multiply(waiting[TOK - 1], TOK - 1, both)
-        add_all(pieces[0], both)
+        quantise(0, 1, prepare(0, 1))
+        quantise(0, 2, prepare(0, 2))
+        first = project(pieces[0], 0)
+        last_tile = prepare(0, 3)
+        multiply(first, 0, both)
+        quantise(0, 3, last_tile)
+        for j in range(1, TOK):
+            multiply(project(pieces[0], j), j, both)
 
-        for piece in pieces[1:]:
-            rotated = piece[4]
-            if rotated:
-                both = products.tile([P, 2, GROUP_HEADS, TOK, HD], F32)
-                for j in range(TOK):
-                    multiply(project(piece, j), j, both)
-                if piece is not pieces[-1]:
-                    add_all(piece, both)
-                else:
-                    result = results.tile([P, GROUP_HEADS, TOK, HD], F32)
-                    for j in range(TOK):
-                        nc.vector.tensor_tensor(
-                            out=result[:, :, j, :], in0=both[:, 0, :, j, :], in1=both[:, 1, :, j, :], op=ADD
-                        )
-                        store_positions(piece, result, j)
-            else:
+        def copy_half(piece, result, first_position):
+            for j in range(first_position, first_position + TOK // 2):
+                acc = project(piece, j)
+                nc.scalar.copy(out=result[:, :, j, :], in_=acc[:].rearrange("p (h d) -> p h d", d=HD))
+
+        fence = keep.tile([P, 1], U32)
+        next_batch = []
+        turn_of = 0
+        for first_piece in range(0, len(pieces), 3):
+            q_piece, v_piece, k_piece = pieces[first_piece : first_piece + 3]
+            v_result = results.tile([P, GROUP_HEADS, TOK, HD], F32, tag="result")
+            for piece in (q_piece, k_piece):
                 result = results.tile([P, GROUP_HEADS, TOK, HD], F32)
-                for j in range(TOK):
-                    acc = project(piece, j)
-                    nc.scalar.copy(out=result[:, :, j, :], in_=acc[:].rearrange("p (h d) -> p h d", d=HD))
-                store(nc.scalar, piece, result)
+                if turn_of > 0:
+                    both = products.tile([P, 2, GROUP_HEADS, TOK, HD], F32)
+                    for j in range(TOK):
+                        multiply(project(piece, j), j, both)
+                copy_half(v_piece, v_result, 0 if piece is q_piece else TOK // 2)
+                if piece is k_piece:
+                    store(nc.scalar, v_piece, v_result, 0, TOK)
+                if turn_of < TOK:
+                    next_batch.append(prepare(1, turn_of))
+                if turn_of == TOK - 1:
+                    for j in range(TOK):
+                        quantise(1, j, next_batch[j])
+                    nc.gpsimd.tensor_copy(out=fence[:], in_=x_codes[:, 1, TOK - 1, PASSES - 1, 0:1])
+                if turn_of < ROTATED_PIECES - 1:
+                    add(nc.gpsimd, both, result, 0, TOK)
+                    store(nc.sync, piece, result, 0, TOK)
+                else:
+                    for j in range(TOK):
+                        add(nc.vector, both, result, j, 1)
+                        store(nc.sync, piece, result, j, 1)
+                turn_of += 1

@@ -93,7 +93,7 @@ def tile_selfattention_pa_kernel(tc, x, w_qkv_words, w_qkv_scales, out_0, out_1,
     with ExitStack() as pools:
         keep = pools.enter_context(tc.tile_pool(name="keep", bufs=1))
         stage = pools.enter_context(tc.tile_pool(name="stage", bufs=4))
-        products = pools.enter_context(tc.tile_pool(name="products", bufs=4))
+        products = pools.enter_context(tc.tile_pool(name="products", bufs=6))
         results = pools.enter_context(tc.tile_pool(name="results", bufs=5))
         banks = pools.enter_context(tc.psum_pool(name="banks", bufs=8))
         pools.enter_context(tc.manual_schedule())
@@ -188,10 +188,10 @@ def tile_selfattention_pa_kernel(tc, x, w_qkv_words, w_qkv_scales, out_0, out_1,
                 )
             return acc
 
-        def multiply(acc, j, both):
+        def multiply(acc, j, both, at=None):
             shape = [P, 2, GROUP_HEADS, PAIRS, 2]
             nc.vector.tensor_tensor(
-                out=both[:, :, :, j, :].rearrange("p w h (i e) -> p w h i e", e=2),
+                out=both[:, :, :, j if at is None else at, :].rearrange("p w h (i e) -> p w h i e", e=2),
                 in0=acc[:].rearrange("p (h i w) -> p w h i", h=GROUP_HEADS, w=2).unsqueeze(4).to_broadcast(shape),
                 in1=table[:, j].unsqueeze(2).to_broadcast(shape),
                 op=MULT,
@@ -233,7 +233,7 @@ def tile_selfattention_pa_kernel(tc, x, w_qkv_words, w_qkv_scales, out_0, out_1,
         fence = keep.tile([P, 1], U32)
         next_batch = []
         turn_of = 0
-        for first_piece in range(0, len(pieces), 3):
+        for first_piece in range(0, len(pieces) - 3, 3):
             q_piece, v_piece, k_piece = pieces[first_piece : first_piece + 3]
             v_result = results.tile([P, GROUP_HEADS, TOK, HD], F32, tag="result")
             for piece in (q_piece, k_piece):
@@ -251,11 +251,52 @@ def tile_selfattention_pa_kernel(tc, x, w_qkv_words, w_qkv_scales, out_0, out_1,
                     for j in range(TOK):
                         quantise(1, j, next_batch[j])
                     nc.gpsimd.tensor_copy(out=fence[:], in_=x_codes[:, 1, TOK - 1, PASSES - 1, 0:1])
-                if turn_of < ROTATED_PIECES - 1:
-                    add(nc.gpsimd, both, result, 0, TOK)
-                    store(nc.sync, piece, result, 0, TOK)
-                else:
-                    for j in range(TOK):
-                        add(nc.vector, both, result, j, 1)
-                        store(nc.sync, piece, result, j, 1)
+                add(nc.gpsimd, both, result, 0, TOK)
+                store(nc.sync, piece, result, 0, TOK)
                 turn_of += 1
+
+        def rotate_part(piece, first, count):
+            terms = products.tile([P, 2, GROUP_HEADS, count, HD], F32, tag="both")
+            for j in range(first, first + count):
+                multiply(project(piece, j), j, terms, j - first)
+            return terms
+
+        def add_part(engine, terms, at, result, first, count):
+            engine.tensor_tensor(
+                out=result[:, :, first : first + count, :],
+                in0=terms[:, 0, :, at : at + count, :],
+                in1=terms[:, 1, :, at : at + count, :],
+                op=ADD,
+            )
+
+        def add_on_tensor(piece, terms, result, j):
+            summed = banks.tile([P, N_TILE], F32, tag="bank")
+            for w in range(2):
+                nc.tensor.matmul(out=summed[:], lhsT=identity[:], rhs=terms[:, w, :, 0, :], start=(w == 0), stop=(w == 1))
+            nc.scalar.copy(out=result[:, :, j, :], in_=summed[:].rearrange("p (h d) -> p h d", d=HD))
+            store(nc.scalar, piece, result, j, 1)
+
+        q_piece, v_piece, k_piece = pieces[len(pieces) - 3 :]
+        v_result = results.tile([P, GROUP_HEADS, TOK, HD], F32, tag="result")
+        q_result = results.tile([P, GROUP_HEADS, TOK, HD], F32, tag="result")
+        k_result = results.tile([P, GROUP_HEADS, TOK, HD], F32, tag="result")
+        q_start = rotate_part(q_piece, 0, 2)
+        add_part(nc.gpsimd, q_start, 0, q_result, 0, 2)
+        store(nc.sync, q_piece, q_result, 0, 2)
+        q_third = rotate_part(q_piece, 2, 1)
+        q_fourth = rotate_part(q_piece, 3, 1)
+        copy_half(v_piece, v_result, 0)
+        copy_half(v_piece, v_result, TOK // 2)
+        store(nc.scalar, v_piece, v_result, 0, TOK)
+        k_start = rotate_part(k_piece, 0, 1)
+        add_part(nc.gpsimd, k_start, 0, k_result, 0, 1)
+        store(nc.sync, k_piece, k_result, 0, 1)
+        k_rest = products.tile([P, 2, GROUP_HEADS, TOK - 1, HD], F32, tag="both")
+        multiply(project(k_piece, 1), 1, k_rest, 0)
+        add_on_tensor(q_piece, q_third, q_result, 2)
+        multiply(project(k_piece, 2), 2, k_rest, 1)
+        multiply(project(k_piece, 3), 3, k_rest, 2)
+        add_on_tensor(q_piece, q_fourth, q_result, 3)
+        for j in range(1, TOK):
+            add_part(nc.vector, k_rest, j - 1, k_result, j, 1)
+            store(nc.sync, k_piece, k_result, j, 1)

@@ -280,23 +280,20 @@ def tile_selfattention_pa_kernel(tc, x, w_qkv_words, w_qkv_scales, out_0, out_1,
         v_result = results.tile([P, GROUP_HEADS, TOK, HD], F32, tag="result")
         q_result = results.tile([P, GROUP_HEADS, TOK, HD], F32, tag="result")
         k_result = results.tile([P, GROUP_HEADS, TOK, HD], F32, tag="result")
-        q_start = rotate_part(q_piece, 0, 2)
-        add_part(nc.gpsimd, q_start, 0, q_result, 0, 2)
-        store(nc.sync, q_piece, q_result, 0, 2)
-        q_third = rotate_part(q_piece, 2, 1)
-        q_fourth = rotate_part(q_piece, 3, 1)
+        q_start = rotate_part(q_piece, 0, TOK - 1)
+        add_part(nc.gpsimd, q_start, 0, q_result, 0, TOK - 1)
+        store(nc.sync, q_piece, q_result, 0, TOK - 1)
+        q_last = rotate_part(q_piece, TOK - 1, 1)
         copy_half(v_piece, v_result, 0)
         copy_half(v_piece, v_result, TOK // 2)
         store(nc.scalar, v_piece, v_result, 0, TOK)
-        k_start = rotate_part(k_piece, 0, 1)
-        add_part(nc.gpsimd, k_start, 0, k_result, 0, 1)
+        k_first = rotate_part(k_piece, 0, 1)
+        add_part(nc.gpsimd, k_first, 0, k_result, 0, 1)
         store(nc.sync, k_piece, k_result, 0, 1)
-        k_rest = products.tile([P, 2, GROUP_HEADS, TOK - 1, HD], F32, tag="both")
-        multiply(project(k_piece, 1), 1, k_rest, 0)
-        add_on_tensor(q_piece, q_third, q_result, 2)
-        multiply(project(k_piece, 2), 2, k_rest, 1)
-        multiply(project(k_piece, 3), 3, k_rest, 2)
-        add_on_tensor(q_piece, q_fourth, q_result, 3)
-        for j in range(1, TOK):
-            add_part(nc.vector, k_rest, j - 1, k_result, j, 1)
+        k_second = rotate_part(k_piece, 1, 1)
+        add_on_tensor(q_piece, q_last, q_result, TOK - 1)
+        k_rest = rotate_part(k_piece, 2, 2)
+        add_on_tensor(k_piece, k_second, k_result, 1)
+        for j in range(2, TOK):
+            add_part(nc.vector, k_rest, j - 2, k_result, j, 1)
             store(nc.sync, k_piece, k_result, j, 1)

@@ -30,6 +30,7 @@ HEAD_GROUPS = H // GROUP_HEADS
 PAIRS = HD // 2
 DOUBLINGS = 6
 assert 2**DOUBLINGS == PAIRS
+STEP = 2 ** (DOUBLINGS // 2)
 ROUND_MAGIC = 1.5 * 2.0**23
 
 ROTATED_PIECES = 2 * B * HEAD_GROUPS
@@ -37,25 +38,29 @@ ROTATED_PIECES = 2 * B * HEAD_GROUPS
 FLOPS = 2 * B * T * D * 3 * E
 
 
-def build_angles(nc, keep):
-    position_int = keep.tile([P, TOK], I32)
-    nc.gpsimd.iota(position_int[:], pattern=[[1, TOK]], base=0, channel_multiplier=TOK)
-    position = keep.tile([P, TOK], F32)
-    nc.vector.tensor_copy(out=position[:], in_=position_int[:])
-
-    freq = keep.tile([P, PAIRS], F32)
-    nc.vector.memset(freq[:, 0:1], 1.0)
-    for doubling in range(DOUBLINGS):
+def build_angles(nc, keep, position):
+    fine = keep.tile([P, STEP], F32)
+    coarse = keep.tile([P, STEP], F32)
+    nc.vector.memset(fine[:, 0:1], 1.0)
+    nc.vector.memset(coarse[:, 0:1], 1.0)
+    for doubling in range(DOUBLINGS // 2):
         have = 2**doubling
-        nc.vector.tensor_scalar_mul(
-            out=freq[:, have : 2 * have], in0=freq[:, 0:have], scalar1=10000.0 ** (-2.0 * have / HD)
-        )
-
+        for (row, stride) in ((fine, 1), (coarse, STEP)):
+            nc.vector.tensor_scalar_mul(
+                out=row[:, have : 2 * have], in0=row[:, 0:have], scalar1=10000.0 ** (-2.0 * have * stride / HD)
+            )
+    freq = keep.tile([P, STEP, STEP], F32)
+    nc.vector.tensor_tensor(
+        out=freq[:],
+        in0=coarse[:].unsqueeze(2).to_broadcast([P, STEP, STEP]),
+        in1=fine[:].unsqueeze(1).to_broadcast([P, STEP, STEP]),
+        op=MULT,
+    )
     shape = [P, TOK, PAIRS]
     turns = keep.tile(shape, F32)
     nc.vector.scalar_tensor_tensor(
         out=turns[:],
-        in0=freq[:].unsqueeze(1).to_broadcast(shape),
+        in0=freq[:].rearrange("p a b -> p (a b)").unsqueeze(1).to_broadcast(shape),
         scalar=1.0 / (2.0 * math.pi),
         in1=position[:].unsqueeze(2).to_broadcast(shape),
         op0=MULT,
@@ -65,26 +70,24 @@ def build_angles(nc, keep):
     nc.vector.tensor_scalar(
         out=whole[:], in0=turns[:], scalar1=ROUND_MAGIC, scalar2=ROUND_MAGIC, op0=ADD, op1=SUBTRACT
     )
-    part = keep.tile(shape, F32)
-    nc.vector.tensor_tensor(out=part[:], in0=turns[:], in1=whole[:], op=SUBTRACT)
+    ready = keep.tile([P, 3, TOK, PAIRS], F32)
+    nc.vector.tensor_tensor(out=ready[:, 2], in0=turns[:], in1=whole[:], op=SUBTRACT)
+    nc.vector.tensor_tensor(out=ready[:, 0], in0=whole[:], in1=turns[:], op=SUBTRACT)
     size = keep.tile(shape, F32)
-    nc.vector.scalar_tensor_tensor(
-        out=size[:], in0=part[:], scalar=-1.0, in1=part[:], op0=MULT, op1=MAX
-    )
-    quarter_less = keep.tile(shape, F32)
-    nc.vector.tensor_scalar(
-        out=quarter_less[:], in0=size[:], scalar1=-1.0, scalar2=0.25, op0=MULT, op1=ADD
-    )
-
-    return part, quarter_less
+    nc.vector.tensor_tensor(out=size[:], in0=ready[:, 0], in1=ready[:, 2], op=MAX)
+    nc.vector.tensor_scalar(out=ready[:, 1], in0=size[:], scalar1=-1.0, scalar2=0.25, op0=MULT, op1=ADD)
+    return ready
 
 
-def build_rotation_table(nc, keep, part, quarter_less):
+def build_rotation_table(nc, keep, ready):
     table = keep.tile([P, TOK, 2, PAIRS, 2], F32)
-    nc.scalar.activation(out=table[:, :, 0, :, 1], in_=part[:], func=SIN, scale=2.0 * math.pi)
-    nc.scalar.activation(out=table[:, :, 1, :, 0], in_=part[:], func=SIN, scale=-2.0 * math.pi)
     for w in range(2):
-        nc.scalar.activation(out=table[:, :, w, :, w], in_=quarter_less[:], func=SIN, scale=2.0 * math.pi)
+        nc.scalar.activation(
+            out=table[:, :, w, :, :],
+            in_=ready[:, 1 - w : 3 - w].rearrange("p e j i -> p j i e"),
+            func=SIN,
+            scale=2.0 * math.pi,
+        )
     return table
 
 
@@ -108,6 +111,10 @@ def tile_selfattention_pa_kernel(tc, x, w_qkv_words, w_qkv_scales, out_0, out_1,
         warm = keep.tile([P, 2], F32)
         nc.vector.memset(warm[:, 0:1], 0.0)
         nc.scalar.activation(out=warm[:, 1:2], in_=warm[:, 0:1], func=SIN)
+        position = keep.tile([P, TOK], F32)
+        nc.gpsimd.iota(
+            position[:], pattern=[[1, TOK]], base=0, channel_multiplier=TOK, allow_small_or_imprecise_dtypes=True
+        )
 
         x_rows = keep.tile([P, B, TOK, D], BF16)
         x_by_partition = x.rearrange("b (p j) k -> b p j k", j=TOK)
@@ -115,34 +122,36 @@ def tile_selfattention_pa_kernel(tc, x, w_qkv_words, w_qkv_scales, out_0, out_1,
         def load_x(b, j):
             nc.sync.dma_start(out=x_rows[:, b, j, :], in_=x_by_partition[b, :, j, :])
 
-        w_words = keep.tile([P, PASSES, 2 * 3 * E], U8, align_bytes=64)
+        w_words = []
+        for chunk in range(3 * HEAD_GROUPS):
+            chunk_words = keep.tile([P, PASSES, 2 * N_TILE], U8, align_bytes=64, name="w_words_%d" % chunk)
+            w_words.append(chunk_words)
         words_by_partition = w_qkv_words.rearrange("g p n -> p g n")
 
         def load_w(chunk):
             cols = slice(2 * N_TILE * chunk, 2 * N_TILE * (chunk + 1))
-            nc.sync.dma_start(
-                out=w_words[:, :, cols].bitcast(I32), in_=words_by_partition[:, :, cols].bitcast(I32)
-            )
+            nc.sync.dma_start(out=w_words[chunk][:].bitcast(I32), in_=words_by_partition[:, :, cols].bitcast(I32))
 
         w_scales = keep.tile([P, PASSES, 3 * E], U8, align_bytes=64)
-        nc.vector.memset(w_scales[:].bitcast(I32), 0)
+        nc.gpsimd.memset(w_scales[:].bitcast(F32), 0.0)
         scales_by_row = w_qkv_scales.rearrange("g q n -> q g n")
 
         chunk_order = [third * HEAD_GROUPS + group for (b, group, dst, third, rotated) in pieces if b == 0]
         load_x(0, 0)
+        load_x(0, 1)
         load_w(chunk_order[0])
         for r in range(4):
             nc.sync.dma_start(out=w_scales[r:P:32].bitcast(I32), in_=scales_by_row[r:16:4].bitcast(I32))
-        for j in range(1, TOK):
+        for j in range(2, TOK):
             load_x(0, j)
         for chunk in chunk_order[1:]:
             load_w(chunk)
         for j in range(TOK):
             load_x(1, j)
 
-        part, quarter_less = build_angles(nc, keep)
         identity = keep.tile([P, P], F32)
         make_identity(nc, identity[:])
+        ready = build_angles(nc, keep, position)
 
         x_codes = keep.tile([P, B, TOK, PASSES, P], U32, align_bytes=64)
         x_scales = keep.tile([P, B, TOK, PASSES, P], U8, align_bytes=64)
@@ -181,7 +190,7 @@ def tile_selfattention_pa_kernel(tc, x, w_qkv_words, w_qkv_scales, out_0, out_1,
                     out=acc[:],
                     lhsT=x_codes[:, b, j, g, :].bitcast(FP8X4),
                     lhsT_scale=x_scales[:, b, j, g, :],
-                    rhs=w_words[:, g, 2 * N_TILE * chunk : 2 * N_TILE * (chunk + 1)].bitcast(FP4X4),
+                    rhs=w_words[chunk][:, g, :].bitcast(FP4X4),
                     rhs_scale=w_scales[:, g, N_TILE * chunk : N_TILE * (chunk + 1)],
                     start=(g == 0),
                     stop=(g == PASSES - 1),
@@ -214,15 +223,20 @@ def tile_selfattention_pa_kernel(tc, x, w_qkv_words, w_qkv_scales, out_0, out_1,
             )
 
         both = products.tile([P, 2, GROUP_HEADS, TOK, HD], F32)
-        quantise(0, 0, prepare(0, 0))
-        table = build_rotation_table(nc, keep, part, quarter_less)
-        quantise(0, 1, prepare(0, 1))
-        quantise(0, 2, prepare(0, 2))
+        tile_0 = prepare(0, 0)
+        tile_1 = prepare(0, 1)
+        quantise(0, 0, tile_0)
+        quantise(0, 1, tile_1)
+        table = build_rotation_table(nc, keep, ready)
         first = project(pieces[0], 0)
-        last_tile = prepare(0, 3)
+        tile_2 = prepare(0, 2)
         multiply(first, 0, both)
-        quantise(0, 3, last_tile)
-        for j in range(1, TOK):
+        quantise(0, 2, tile_2)
+        second = project(pieces[0], 1)
+        tile_3 = prepare(0, 3)
+        multiply(second, 1, both)
+        quantise(0, 3, tile_3)
+        for j in range(2, TOK):
             multiply(project(pieces[0], j), j, both)
 
         def copy_half(piece, result, first_position):

@@ -247,6 +247,7 @@ def tile_selfattention_pa_kernel(tc, x, w_qkv_words, w_qkv_scales, out_0, out_1,
         fence = keep.tile([P, 1], U32)
         next_batch = []
         turn_of = 0
+        early = []
         for first_piece in range(0, len(pieces) - 3, 3):
             q_piece, v_piece, k_piece = pieces[first_piece : first_piece + 3]
             v_result = results.tile([P, GROUP_HEADS, TOK, HD], F32, tag="result")
@@ -255,7 +256,9 @@ def tile_selfattention_pa_kernel(tc, x, w_qkv_words, w_qkv_scales, out_0, out_1,
                 if turn_of > 0:
                     both = products.tile([P, 2, GROUP_HEADS, TOK, HD], F32)
                     for j in range(TOK):
-                        multiply(project(piece, j), j, both)
+                        multiply(early.pop(0) if early else project(piece, j), j, both)
+                else:
+                    early.extend([project(k_piece, 0), project(k_piece, 1)])
                 copy_half(v_piece, v_result, 0 if piece is q_piece else TOK // 2)
                 if piece is k_piece:
                     store(nc.scalar, v_piece, v_result, 0, TOK)
@@ -305,8 +308,8 @@ def tile_selfattention_pa_kernel(tc, x, w_qkv_words, w_qkv_scales, out_0, out_1,
         add_part(nc.gpsimd, k_first, 0, k_result, 0, 1)
         store(nc.sync, k_piece, k_result, 0, 1)
         k_second = rotate_part(k_piece, 1, 1)
-        add_on_tensor(q_piece, q_last, q_result, TOK - 1)
         k_rest = rotate_part(k_piece, 2, 2)
+        add_on_tensor(q_piece, q_last, q_result, TOK - 1)
         add_on_tensor(k_piece, k_second, k_result, 1)
         for j in range(2, TOK):
             add_part(nc.vector, k_rest, j - 2, k_result, j, 1)

@@ -132,8 +132,10 @@ def tile_selfattention_pa_kernel(tc, x, w_qkv_words, w_qkv_scales, out_0, out_1,
             cols = slice(2 * N_TILE * chunk, 2 * N_TILE * (chunk + 1))
             nc.sync.dma_start(out=w_words[chunk][:].bitcast(I32), in_=words_by_partition[:, :, cols].bitcast(I32))
 
-        w_scales = keep.tile([P, PASSES, 3 * E], U8, align_bytes=64)
-        nc.gpsimd.memset(w_scales[:].bitcast(F32), 0.0)
+        first_scales = keep.tile([P, PASSES, N_TILE], U8, align_bytes=64)
+        other_scales = keep.tile([P, PASSES, 3 * E - N_TILE], U8, align_bytes=64)
+        nc.gpsimd.memset(first_scales[:].bitcast(F32), 0.0)
+        nc.gpsimd.memset(other_scales[:].bitcast(F32), 0.0)
         scales_by_row = w_qkv_scales.rearrange("g q n -> q g n")
 
         chunk_order = [third * HEAD_GROUPS + group for (b, group, dst, third, rotated) in pieces if b == 0]
@@ -141,9 +143,15 @@ def tile_selfattention_pa_kernel(tc, x, w_qkv_words, w_qkv_scales, out_0, out_1,
         load_x(0, 1)
         load_w(chunk_order[0])
         for r in range(4):
-            nc.sync.dma_start(out=w_scales[r:P:32].bitcast(I32), in_=scales_by_row[r:16:4].bitcast(I32))
+            nc.sync.dma_start(
+                out=first_scales[r:P:32].bitcast(I32), in_=scales_by_row[r:16:4, :, 0:N_TILE].bitcast(I32)
+            )
         for j in range(2, TOK):
             load_x(0, j)
+        for r in range(4):
+            nc.sync.dma_start(
+                out=other_scales[r:P:32].bitcast(I32), in_=scales_by_row[r:16:4, :, N_TILE : 3 * E].bitcast(I32)
+            )
         for chunk in chunk_order[1:]:
             load_w(chunk)
         for j in range(TOK):
@@ -191,7 +199,9 @@ def tile_selfattention_pa_kernel(tc, x, w_qkv_words, w_qkv_scales, out_0, out_1,
                     lhsT=x_codes[:, b, j, g, :].bitcast(FP8X4),
                     lhsT_scale=x_scales[:, b, j, g, :],
                     rhs=w_words[chunk][:, g, :].bitcast(FP4X4),
-                    rhs_scale=w_scales[:, g, N_TILE * chunk : N_TILE * (chunk + 1)],
+                    rhs_scale=(
+                        first_scales[:, g, :] if chunk == 0 else other_scales[:, g, N_TILE * (chunk - 1) : N_TILE * chunk]
+                    ),
                     start=(g == 0),
                     stop=(g == PASSES - 1),
                 )

@@ -98,7 +98,9 @@ def tile_selfattention_pa_kernel(tc, x, w_qkv_words, w_qkv_scales, out_0, out_1,
         stage = pools.enter_context(tc.tile_pool(name="stage", bufs=4))
         products = pools.enter_context(tc.tile_pool(name="products", bufs=6))
         results = pools.enter_context(tc.tile_pool(name="results", bufs=5))
-        banks = pools.enter_context(tc.psum_pool(name="banks", bufs=8))
+        banks = pools.enter_context(tc.psum_pool(name="banks", bufs=7))
+        fixed = pools.enter_context(tc.psum_pool(name="fixed", bufs=1))
+        copies = pools.enter_context(tc.tile_pool(name="copies", bufs=3))
         pools.enter_context(tc.manual_schedule())
 
         pieces = [
@@ -216,6 +218,34 @@ def tile_selfattention_pa_kernel(tc, x, w_qkv_words, w_qkv_scales, out_0, out_1,
                 op=MULT,
             )
 
+        late_table = fixed.tile([P, 2, 2 * HD], F32)
+
+        def copy_table():
+            for w in range(2):
+                nc.tensor.matmul(
+                    out=late_table[:, w, :],
+                    lhsT=identity[:],
+                    rhs=table[:, 2:TOK, w].rearrange("p c i e -> p c (i e)"),
+                    start=True,
+                    stop=True,
+                )
+
+        def fetch_late(piece):
+            values = copies.tile([P, GROUP_HEADS, 2, HD], F32)
+            for c in range(2):
+                acc = project(piece, 2 + c)
+                nc.scalar.copy(out=values[:, :, c, :], in_=acc[:].rearrange("p (h d) -> p h d", d=HD))
+            return values
+
+        def multiply_late(values, both, at):
+            shape = [P, 2, GROUP_HEADS, 2 * PAIRS, 2]
+            nc.vector.tensor_tensor(
+                out=both[:, :, :, at : at + 2, :].rearrange("p w h c (i e) -> p w h (c i) e", e=2),
+                in0=values[:].rearrange("p h c (i w) -> p w h (c i)", w=2).unsqueeze(4).to_broadcast(shape),
+                in1=late_table[:].rearrange("p w (m e) -> p w m e", e=2).unsqueeze(2).to_broadcast(shape),
+                op=MULT,
+            )
+
         def store(queue, piece, result, first, count):
             b, group, dst, third, rotated = piece
             heads = slice(GROUP_HEADS * group, GROUP_HEADS * (group + 1))
@@ -258,6 +288,7 @@ def tile_selfattention_pa_kernel(tc, x, w_qkv_words, w_qkv_scales, out_0, out_1,
         next_batch = []
         turn_of = 0
         early = []
+        rotated_pieces = [piece for piece in pieces[: len(pieces) - 3] if piece[4]]
         for first_piece in range(0, len(pieces) - 3, 3):
             q_piece, v_piece, k_piece = pieces[first_piece : first_piece + 3]
             v_result = results.tile([P, GROUP_HEADS, TOK, HD], F32, tag="result")
@@ -265,10 +296,17 @@ def tile_selfattention_pa_kernel(tc, x, w_qkv_words, w_qkv_scales, out_0, out_1,
                 result = results.tile([P, GROUP_HEADS, TOK, HD], F32)
                 if turn_of > 0:
                     both = products.tile([P, 2, GROUP_HEADS, TOK, HD], F32)
-                    for j in range(TOK):
-                        multiply(early.pop(0) if early else project(piece, j), j, both)
-                else:
-                    early.extend([project(k_piece, 0), project(k_piece, 1)])
+                    if not early:
+                        early.extend([project(piece, 0), project(piece, 1), fetch_late(piece)])
+                    multiply(early[0], 0, both)
+                    multiply(early[1], 1, both)
+                    multiply_late(early[2], both, 2)
+                    early.clear()
+                if turn_of + 1 < len(rotated_pieces) and turn_of + 1 != TOK:
+                    ahead = rotated_pieces[turn_of + 1]
+                    early.extend([project(ahead, 0), project(ahead, 1), fetch_late(ahead)])
+                if turn_of == 0:
+                    copy_table()
                 copy_half(v_piece, v_result, 0 if piece is q_piece else TOK // 2)
                 if piece is k_piece:
                     store(nc.scalar, v_piece, v_result, 0, TOK)
@@ -296,21 +334,28 @@ def tile_selfattention_pa_kernel(tc, x, w_qkv_words, w_qkv_scales, out_0, out_1,
                 op=ADD,
             )
 
-        def add_on_tensor(piece, terms, result, j):
+        def add_on_tensor(piece, terms, at, result, j):
             summed = banks.tile([P, N_TILE], F32, tag="bank")
             for w in range(2):
-                nc.tensor.matmul(out=summed[:], lhsT=identity[:], rhs=terms[:, w, :, 0, :], start=(w == 0), stop=(w == 1))
+                nc.tensor.matmul(out=summed[:], lhsT=identity[:], rhs=terms[:, w, :, at, :], start=(w == 0), stop=(w == 1))
             nc.scalar.copy(out=result[:, :, j, :], in_=summed[:].rearrange("p (h d) -> p h d", d=HD))
             store(nc.scalar, piece, result, j, 1)
+
+        def rotate_late(piece):
+            terms = products.tile([P, 2, GROUP_HEADS, 2, HD], F32, tag="both")
+            multiply_late(fetch_late(piece), terms, 0)
+            return terms
 
         q_piece, v_piece, k_piece = pieces[len(pieces) - 3 :]
         v_result = results.tile([P, GROUP_HEADS, TOK, HD], F32, tag="result")
         q_result = results.tile([P, GROUP_HEADS, TOK, HD], F32, tag="result")
         k_result = results.tile([P, GROUP_HEADS, TOK, HD], F32, tag="result")
-        q_start = rotate_part(q_piece, 0, TOK - 1)
-        add_part(nc.gpsimd, q_start, 0, q_result, 0, TOK - 1)
-        store(nc.sync, q_piece, q_result, 0, TOK - 1)
-        q_last = rotate_part(q_piece, TOK - 1, 1)
+        q_start = rotate_part(q_piece, 0, 2)
+        add_part(nc.gpsimd, q_start, 0, q_result, 0, 2)
+        store(nc.sync, q_piece, q_result, 0, 2)
+        q_rest = rotate_late(q_piece)
+        add_part(nc.gpsimd, q_rest, 0, q_result, 2, 1)
+        store(nc.sync, q_piece, q_result, 2, 1)
         copy_half(v_piece, v_result, 0)
         copy_half(v_piece, v_result, TOK // 2)
         store(nc.scalar, v_piece, v_result, 0, TOK)
@@ -318,9 +363,9 @@ def tile_selfattention_pa_kernel(tc, x, w_qkv_words, w_qkv_scales, out_0, out_1,
         add_part(nc.gpsimd, k_first, 0, k_result, 0, 1)
         store(nc.sync, k_piece, k_result, 0, 1)
         k_second = rotate_part(k_piece, 1, 1)
-        k_rest = rotate_part(k_piece, 2, 2)
-        add_on_tensor(q_piece, q_last, q_result, TOK - 1)
-        add_on_tensor(k_piece, k_second, k_result, 1)
+        k_rest = rotate_late(k_piece)
+        add_on_tensor(q_piece, q_rest, 1, q_result, TOK - 1)
+        add_on_tensor(k_piece, k_second, 0, k_result, 1)
         for j in range(2, TOK):
             add_part(nc.vector, k_rest, j - 2, k_result, j, 1)
             store(nc.sync, k_piece, k_result, j, 1)

@@ -262,7 +262,10 @@ def tile_selfattention_pa_kernel(tc, x, w_qkv_words, w_qkv_scales, out_0, out_1,
                 op=ADD,
             )
 
-        both = products.tile([P, 2, GROUP_HEADS, TOK, HD], F32)
+        first_halves = []
+        for half in range(2):
+            both = products.tile([P, 2, GROUP_HEADS, TOK // 2, HD], F32)
+            first_halves.append(both)
         tile_0 = prepare(0, 0)
         tile_1 = prepare(0, 1)
         quantise(0, 0, tile_0)
@@ -270,14 +273,14 @@ def tile_selfattention_pa_kernel(tc, x, w_qkv_words, w_qkv_scales, out_0, out_1,
         table = build_rotation_table(nc, keep, ready)
         first = project(pieces[0], 0)
         tile_2 = prepare(0, 2)
-        multiply(first, 0, both)
+        multiply(first, 0, first_halves[0], 0)
         quantise(0, 2, tile_2)
         second = project(pieces[0], 1)
         tile_3 = prepare(0, 3)
-        multiply(second, 1, both)
+        multiply(second, 1, first_halves[0], 1)
         quantise(0, 3, tile_3)
         for j in range(2, TOK):
-            multiply(project(pieces[0], j), j, both)
+            multiply(project(pieces[0], j), j, first_halves[1], j - 2)
 
         def copy_half(piece, result, first_position):
             for j in range(first_position, first_position + TOK // 2):
@@ -316,7 +319,17 @@ def tile_selfattention_pa_kernel(tc, x, w_qkv_words, w_qkv_scales, out_0, out_1,
                     for j in range(TOK):
                         quantise(1, j, next_batch[j])
                     nc.gpsimd.tensor_copy(out=fence[:], in_=x_codes[:, 1, TOK - 1, PASSES - 1, 0:1])
-                add(nc.gpsimd, both, result, 0, TOK)
+                if turn_of == 0:
+                    nc.gpsimd.tensor_copy(out=fence[:], in_=x_codes[:, 0, TOK - 1, PASSES - 1, 0:1])
+                    for half in range(2):
+                        nc.gpsimd.tensor_tensor(
+                            out=result[:, :, 2 * half : 2 * half + 2, :],
+                            in0=first_halves[half][:, 0],
+                            in1=first_halves[half][:, 1],
+                            op=ADD,
+                        )
+                else:
+                    add(nc.gpsimd, both, result, 0, TOK)
                 store(nc.sync, piece, result, 0, TOK)
                 turn_of += 1
 

@@ -137,7 +137,6 @@ def tile_selfattention_pa_kernel(tc, x, w_qkv_words, w_qkv_scales, out_0, out_1,
         first_scales = keep.tile([P, PASSES, N_TILE], U8, align_bytes=64)
         other_scales = keep.tile([P, PASSES, 3 * E - N_TILE], U8, align_bytes=64)
         nc.gpsimd.memset(first_scales[:].bitcast(F32), 0.0)
-        nc.gpsimd.memset(other_scales[:].bitcast(F32), 0.0)
         scales_by_row = w_qkv_scales.rearrange("g q n -> q g n")
 
         chunk_order = [third * HEAD_GROUPS + group for (b, group, dst, third, rotated) in pieces if b == 0]
@@ -150,14 +149,18 @@ def tile_selfattention_pa_kernel(tc, x, w_qkv_words, w_qkv_scales, out_0, out_1,
             )
         for j in range(2, TOK):
             load_x(0, j)
-        for r in range(4):
-            nc.sync.dma_start(
-                out=other_scales[r:P:32].bitcast(I32), in_=scales_by_row[r:16:4, :, N_TILE : 3 * E].bitcast(I32)
-            )
-        for chunk in chunk_order[1:]:
+        for chunk in chunk_order[1:3]:
             load_w(chunk)
-        for j in range(TOK):
-            load_x(1, j)
+
+        def load_the_rest():
+            for r in range(4):
+                nc.sync.dma_start(
+                    out=other_scales[r:P:32].bitcast(I32), in_=scales_by_row[r:16:4, :, N_TILE : 3 * E].bitcast(I32)
+                )
+            for chunk in chunk_order[3:]:
+                load_w(chunk)
+            for j in range(TOK):
+                load_x(1, j)
 
         identity = keep.tile([P, P], F32)
         make_identity(nc, identity[:])
@@ -270,6 +273,8 @@ def tile_selfattention_pa_kernel(tc, x, w_qkv_words, w_qkv_scales, out_0, out_1,
         tile_1 = prepare(0, 1)
         quantise(0, 0, tile_0)
         quantise(0, 1, tile_1)
+        nc.vector.memset(other_scales[:].bitcast(I32), 0)
+        load_the_rest()
         table = build_rotation_table(nc, keep, ready)
         first = project(pieces[0], 0)
         tile_2 = prepare(0, 2)

import math
from contextlib import ExitStack

import concourse.mybir as mybir
from concourse.masks import make_identity

F32 = mybir.dt.float32
BF16 = mybir.dt.bfloat16
I32 = mybir.dt.int32
U32 = mybir.dt.uint32
U8 = mybir.dt.uint8
FP8X4 = mybir.dt.float8_e4m3fn_x4
FP4X4 = mybir.dt.float4_e2m1fn_x4
MULT = mybir.AluOpType.mult
ADD = mybir.AluOpType.add
SUBTRACT = mybir.AluOpType.subtract
MAX = mybir.AluOpType.max
SIN = mybir.ActivationFunctionType.Sin

B, T, D, H, HD = 2, 512, 1024, 8, 128
E = H * HD
P = 128
PACK = 4
K_PASS = P * PACK
PASSES = D // K_PASS
TOK = T // P
N_TILE = 512
GROUP_HEADS = N_TILE // HD
HEAD_GROUPS = H // GROUP_HEADS
PAIRS = HD // 2
DOUBLINGS = 6
assert 2**DOUBLINGS == PAIRS
STEP = 2 ** (DOUBLINGS // 2)
ROUND_MAGIC = 1.5 * 2.0**23

ROTATED_PIECES = 2 * B * HEAD_GROUPS

FLOPS = 2 * B * T * D * 3 * E


def build_angles(nc, keep, position):
    fine = keep.tile([P, STEP], F32)
    coarse = keep.tile([P, STEP], F32)
    nc.vector.memset(fine[:, 0:1], 1.0)
    nc.vector.memset(coarse[:, 0:1], 1.0)
    for doubling in range(DOUBLINGS // 2):
        have = 2**doubling
        for (row, stride) in ((fine, 1), (coarse, STEP)):
            nc.vector.tensor_scalar_mul(
                out=row[:, have : 2 * have], in0=row[:, 0:have], scalar1=10000.0 ** (-2.0 * have * stride / HD)
            )
    freq = keep.tile([P, STEP, STEP], F32)
    nc.vector.tensor_tensor(
        out=freq[:],
        in0=coarse[:].unsqueeze(2).to_broadcast([P, STEP, STEP]),
        in1=fine[:].unsqueeze(1).to_broadcast([P, STEP, STEP]),
        op=MULT,
    )
    shape = [P, TOK, PAIRS]
    turns = keep.tile(shape, F32)
    nc.vector.scalar_tensor_tensor(
        out=turns[:],
        in0=freq[:].rearrange("p a b -> p (a b)").unsqueeze(1).to_broadcast(shape),
        scalar=1.0 / (2.0 * math.pi),
        in1=position[:].unsqueeze(2).to_broadcast(shape),
        op0=MULT,
        op1=MULT,
    )
    whole = keep.tile(shape, F32)
    nc.vector.tensor_scalar(
        out=whole[:], in0=turns[:], scalar1=ROUND_MAGIC, scalar2=ROUND_MAGIC, op0=ADD, op1=SUBTRACT
    )
    ready = keep.tile([P, 3, TOK, PAIRS], F32)
    nc.vector.tensor_tensor(out=ready[:, 2], in0=turns[:], in1=whole[:], op=SUBTRACT)
    nc.vector.tensor_tensor(out=ready[:, 0], in0=whole[:], in1=turns[:], op=SUBTRACT)
    size = keep.tile(shape, F32)
    nc.vector.tensor_tensor(out=size[:], in0=ready[:, 0], in1=ready[:, 2], op=MAX)
    nc.vector.tensor_scalar(out=ready[:, 1], in0=size[:], scalar1=-1.0, scalar2=0.25, op0=MULT, op1=ADD)
    return ready


def build_rotation_table(nc, keep, ready):
    table = keep.tile([P, TOK, 2, PAIRS, 2], F32)
    for w in range(2):
        nc.scalar.activation(
            out=table[:, :, w, :, :],
            in_=ready[:, 1 - w : 3 - w].rearrange("p e j i -> p j i e"),
            func=SIN,
            scale=2.0 * math.pi,
        )
    return table


def tile_selfattention_pa_kernel(tc, x, w_qkv_words, w_qkv_scales, out_0, out_1, out_2):
    nc = tc.nc
    with ExitStack() as pools:
        keep = pools.enter_context(tc.tile_pool(name="keep", bufs=1))
        stage = pools.enter_context(tc.tile_pool(name="stage", bufs=4))
        products = pools.enter_context(tc.tile_pool(name="products", bufs=6))
        results = pools.enter_context(tc.tile_pool(name="results", bufs=5))
        banks = pools.enter_context(tc.psum_pool(name="banks", bufs=7))
        fixed = pools.enter_context(tc.psum_pool(name="fixed", bufs=1))
        copies = pools.enter_context(tc.tile_pool(name="copies", bufs=3))
        pools.enter_context(tc.manual_schedule())

        pieces = [
            (b, group, dst, third, rotated)
            for b in range(B)
            for group in range(HEAD_GROUPS)
            for (dst, third, rotated) in ((out_0, 0, True), (out_2, 2, False), (out_1, 1, True))
        ]

        warm = keep.tile([P, 2], F32)
        nc.vector.memset(warm[:, 0:1], 0.0)
        nc.scalar.activation(out=warm[:, 1:2], in_=warm[:, 0:1], func=SIN)
        position = keep.tile([P, TOK], F32)
        nc.gpsimd.iota(
            position[:], pattern=[[1, TOK]], base=0, channel_multiplier=TOK, allow_small_or_imprecise_dtypes=True
        )

        x_rows = keep.tile([P, B, TOK, D], BF16)
        x_by_partition = x.rearrange("b (p j) k -> b p j k", j=TOK)

        def load_x(b, j):
            nc.sync.dma_start(out=x_rows[:, b, j, :], in_=x_by_partition[b, :, j, :])

        w_words = []
        for chunk in range(3 * HEAD_GROUPS):
            chunk_words = keep.tile([P, PASSES, 2 * N_TILE], U8, align_bytes=64, name="w_words_%d" % chunk)
            w_words.append(chunk_words)
        words_by_partition = w_qkv_words.rearrange("g p n -> p g n")

        def load_w(chunk):
            cols = slice(2 * N_TILE * chunk, 2 * N_TILE * (chunk + 1))
            nc.sync.dma_start(out=w_words[chunk][:].bitcast(I32), in_=words_by_partition[:, :, cols].bitcast(I32))

        first_scales = keep.tile([P, PASSES, N_TILE], U8, align_bytes=64)
        other_scales = keep.tile([P, PASSES, 3 * E - N_TILE], U8, align_bytes=64)
        nc.gpsimd.memset(first_scales[:].bitcast(F32), 0.0)
        scales_by_row = w_qkv_scales.rearrange("g q n -> q g n")

        chunk_order = [third * HEAD_GROUPS + group for (b, group, dst, third, rotated) in pieces if b == 0]
        load_x(0, 0)
        load_x(0, 1)
        load_w(chunk_order[0])
        for r in range(4):
            nc.sync.dma_start(
                out=first_scales[r:P:32].bitcast(I32), in_=scales_by_row[r:16:4, :, 0:N_TILE].bitcast(I32)
            )
        for j in range(2, TOK):
            load_x(0, j)
        for chunk in chunk_order[1:3]:
            load_w(chunk)

        def load_the_rest():
            for r in range(4):
                nc.sync.dma_start(
                    out=other_scales[r:P:32].bitcast(I32), in_=scales_by_row[r:16:4, :, N_TILE : 3 * E].bitcast(I32)
                )
            for chunk in chunk_order[3:]:
                load_w(chunk)
            for j in range(TOK):
                load_x(1, j)

        identity = keep.tile([P, P], F32)
        make_identity(nc, identity[:])
        ready = build_angles(nc, keep, position)

        x_codes = keep.tile([P, B, TOK, PASSES, P], U32, align_bytes=64)
        x_scales = keep.tile([P, B, TOK, PASSES, P], U8, align_bytes=64)

        def prepare(b, j):
            words = x_rows[:, b, j, :].bitcast(F32)
            turned = banks.tile([P, PASSES, 2, P], F32, tag="bank")
            for g in range(PASSES):
                for u in range(2):
                    nc.tensor.transpose(
                        turned[:, g, u, :], words[:, 2 * P * g + u : 2 * P * (g + 1) : 2], identity[:]
                    )
            grouped = stage.tile([P, PASSES, P, PACK], BF16, align_bytes=64)
            nc.scalar.copy(
                out=grouped[:]
                .rearrange("p g r t -> p (g r t)")
                .bitcast(F32)
                .rearrange("p (g r u) -> p g r u", g=PASSES, u=2),
                in_=turned[:].rearrange("p g u r -> p g r u"),
            )
            return grouped

        def quantise(b, j, grouped):
            nc.vector.quantize_mx(
                out=x_codes[:, b, j].rearrange("p g r -> p (g r)").bitcast(FP8X4),
                scales=x_scales[:, b, j].rearrange("p g r -> p (g r)"),
                in_=grouped[:].rearrange("p g r t -> p (g r t)"),
            )

        def project(piece, j):
            b, group, dst, third, rotated = piece
            chunk = third * HEAD_GROUPS + group
            acc = banks.tile([P, N_TILE], F32, tag="bank")
            for g in range(PASSES):
                nc.tensor.matmul_mx(
                    out=acc[:],
                    lhsT=x_codes[:, b, j, g, :].bitcast(FP8X4),
                    lhsT_scale=x_scales[:, b, j, g, :],
                    rhs=w_words[chunk][:, g, :].bitcast(FP4X4),
                    rhs_scale=(
                        first_scales[:, g, :] if chunk == 0 else other_scales[:, g, N_TILE * (chunk - 1) : N_TILE * chunk]
                    ),
                    start=(g == 0),
                    stop=(g == PASSES - 1),
                )
            return acc

        def multiply(acc, j, both, at=None):
            shape = [P, 2, GROUP_HEADS, PAIRS, 2]
            nc.vector.tensor_tensor(
                out=both[:, :, :, j if at is None else at, :].rearrange("p w h (i e) -> p w h i e", e=2),
                in0=acc[:].rearrange("p (h i w) -> p w h i", h=GROUP_HEADS, w=2).unsqueeze(4).to_broadcast(shape),
                in1=table[:, j].unsqueeze(2).to_broadcast(shape),
                op=MULT,
            )

        late_table = fixed.tile([P, 2, 2 * HD], F32)

        def copy_table():
            for w in range(2):
                nc.tensor.matmul(
                    out=late_table[:, w, :],
                    lhsT=identity[:],
                    rhs=table[:, 2:TOK, w].rearrange("p c i e -> p c (i e)"),
                    start=True,
                    stop=True,
                )

        def fetch_late(piece):
            values = copies.tile([P, GROUP_HEADS, 2, HD], F32)
            for c in range(2):
                acc = project(piece, 2 + c)
                nc.scalar.copy(out=values[:, :, c, :], in_=acc[:].rearrange("p (h d) -> p h d", d=HD))
            return values

        def multiply_late(values, both, at):
            shape = [P, 2, GROUP_HEADS, 2 * PAIRS, 2]
            nc.vector.tensor_tensor(
                out=both[:, :, :, at : at + 2, :].rearrange("p w h c (i e) -> p w h (c i) e", e=2),
                in0=values[:].rearrange("p h c (i w) -> p w h (c i)", w=2).unsqueeze(4).to_broadcast(shape),
                in1=late_table[:].rearrange("p w (m e) -> p w m e", e=2).unsqueeze(2).to_broadcast(shape),
                op=MULT,
            )

        def store(queue, piece, result, first, count):
            b, group, dst, third, rotated = piece
            heads = slice(GROUP_HEADS * group, GROUP_HEADS * (group + 1))
            queue.dma_start(
                out=dst[b, heads].rearrange("h (p j) d -> p h j d", j=TOK)[:, :, first : first + count, :],
                in_=result[:, :, first : first + count, :],
            )

        def add(engine, both, result, first, count):
            engine.tensor_tensor(
                out=result[:, :, first : first + count, :],
                in0=both[:, 0, :, first : first + count, :],
                in1=both[:, 1, :, first : first + count, :],
                op=ADD,
            )

        first_halves = []
        for half in range(2):
            both = products.tile([P, 2, GROUP_HEADS, TOK // 2, HD], F32)
            first_halves.append(both)
        tile_0 = prepare(0, 0)
        tile_1 = prepare(0, 1)
        quantise(0, 0, tile_0)
        quantise(0, 1, tile_1)
        nc.vector.memset(other_scales[:].bitcast(I32), 0)
        load_the_rest()
        table = build_rotation_table(nc, keep, ready)
        first = project(pieces[0], 0)
        tile_2 = prepare(0, 2)
        multiply(first, 0, first_halves[0], 0)
        quantise(0, 2, tile_2)
        second = project(pieces[0], 1)
        tile_3 = prepare(0, 3)
        multiply(second, 1, first_halves[0], 1)
        quantise(0, 3, tile_3)
        for j in range(2, TOK):
            multiply(project(pieces[0], j), j, first_halves[1], j - 2)

        def copy_half(piece, result, first_position):
            for j in range(first_position, first_position + TOK // 2):
                acc = project(piece, j)
                nc.scalar.copy(out=result[:, :, j, :], in_=acc[:].rearrange("p (h d) -> p h d", d=HD))

        fence = keep.tile([P, 1], U32)
        next_batch = []
        turn_of = 0
        early = []
        rotated_pieces = [piece for piece in pieces[: len(pieces) - 3] if piece[4]]
        for first_piece in range(0, len(pieces) - 3, 3):
            q_piece, v_piece, k_piece = pieces[first_piece : first_piece + 3]
            v_result = results.tile([P, GROUP_HEADS, TOK, HD], F32, tag="result")
            for piece in (q_piece, k_piece):
                result = results.tile([P, GROUP_HEADS, TOK, HD], F32)
                if turn_of > 0:
                    both = products.tile([P, 2, GROUP_HEADS, TOK, HD], F32)
                    if not early:
                        early.extend([project(piece, 0), project(piece, 1), fetch_late(piece)])
                    multiply(early[0], 0, both)
                    multiply(early[1], 1, both)
                    multiply_late(early[2], both, 2)
                    early.clear()
                if turn_of + 1 < len(rotated_pieces) and turn_of + 1 != TOK:
                    ahead = rotated_pieces[turn_of + 1]
                    early.extend([project(ahead, 0), project(ahead, 1), fetch_late(ahead)])
                if turn_of == 0:
                    copy_table()
                copy_half(v_piece, v_result, 0 if piece is q_piece else TOK // 2)
                if piece is k_piece:
                    store(nc.scalar, v_piece, v_result, 0, TOK)
                if turn_of < TOK:
                    next_batch.append(prepare(1, turn_of))
                if turn_of == TOK - 1:
                    for j in range(TOK):
                        quantise(1, j, next_batch[j])
                    nc.gpsimd.tensor_copy(out=fence[:], in_=x_codes[:, 1, TOK - 1, PASSES - 1, 0:1])
                if turn_of == 0:
                    nc.gpsimd.tensor_copy(out=fence[:], in_=x_codes[:, 0, TOK - 1, PASSES - 1, 0:1])
                    for half in range(2):
                        nc.gpsimd.tensor_tensor(
                            out=result[:, :, 2 * half : 2 * half + 2, :],
                            in0=first_halves[half][:, 0],
                            in1=first_halves[half][:, 1],
                            op=ADD,
                        )
                else:
                    add(nc.gpsimd, both, result, 0, TOK)
                store(nc.sync, piece, result, 0, TOK)
                turn_of += 1

        def rotate_part(piece, first, count):
            terms = products.tile([P, 2, GROUP_HEADS, count, HD], F32, tag="both")
            for j in range(first, first + count):
                multiply(project(piece, j), j, terms, j - first)
            return terms

        def add_part(engine, terms, at, result, first, count):
            engine.tensor_tensor(
                out=result[:, :, first : first + count, :],
                in0=terms[:, 0, :, at : at + count, :],
                in1=terms[:, 1, :, at : at + count, :],
                op=ADD,
            )

        def add_on_tensor(piece, terms, at, result, j):
            summed = banks.tile([P, N_TILE], F32, tag="bank")
            for w in range(2):
                nc.tensor.matmul(out=summed[:], lhsT=identity[:], rhs=terms[:, w, :, at, :], start=(w == 0), stop=(w == 1))
            nc.scalar.copy(out=result[:, :, j, :], in_=summed[:].rearrange("p (h d) -> p h d", d=HD))
            store(nc.scalar, piece, result, j, 1)

        def rotate_late(piece):
            terms = products.tile([P, 2, GROUP_HEADS, 2, HD], F32, tag="both")
            multiply_late(fetch_late(piece), terms, 0)
            return terms

        q_piece, v_piece, k_piece = pieces[len(pieces) - 3 :]
        v_result = results.tile([P, GROUP_HEADS, TOK, HD], F32, tag="result")
        q_result = results.tile([P, GROUP_HEADS, TOK, HD], F32, tag="result")
        k_result = results.tile([P, GROUP_HEADS, TOK, HD], F32, tag="result")
        q_start = rotate_part(q_piece, 0, 2)
        add_part(nc.gpsimd, q_start, 0, q_result, 0, 2)
        store(nc.sync, q_piece, q_result, 0, 2)
        q_rest = rotate_late(q_piece)
        add_part(nc.gpsimd, q_rest, 0, q_result, 2, 1)
        store(nc.sync, q_piece, q_result, 2, 1)
        copy_half(v_piece, v_result, 0)
        copy_half(v_piece, v_result, TOK // 2)
        store(nc.scalar, v_piece, v_result, 0, TOK)
        k_first = rotate_part(k_piece, 0, 1)
        add_part(nc.gpsimd, k_first, 0, k_result, 0, 1)
        store(nc.sync, k_piece, k_result, 0, 1)
        k_second = rotate_part(k_piece, 1, 1)
        k_rest = rotate_late(k_piece)
        add_on_tensor(q_piece, q_rest, 1, q_result, TOK - 1)
        add_on_tensor(k_piece, k_second, 0, k_result, 1)
        for j in range(2, TOK):
            add_part(nc.vector, k_rest, j - 2, k_result, j, 1)
            store(nc.sync, k_piece, k_result, j, 1)
